import numpy as np
import ml_dtypes


def mxq(x, axis, fmt="e4m3"):
    dtype, down = {"e4m3": (ml_dtypes.float8_e4m3fn, 7), "e5m2": (ml_dtypes.float8_e5m2, 14)}[fmt]
    v = np.moveaxis(np.asarray(x, np.float32).astype(ml_dtypes.bfloat16).astype(np.float64), axis, -1)
    blocks = v.reshape(v.shape[:-1] + (-1, 32))
    amax = np.abs(blocks).max(-1, keepdims=True)
    byte = np.maximum(np.where(amax > 0, np.frexp(amax)[1] - 1 + 127, 0) - down, 1)
    scale = np.exp2(byte - 127.0)
    codes = (blocks / scale).astype(np.float32).astype(dtype).astype(np.float64)
    return np.moveaxis((codes * scale).reshape(v.shape), -1, axis)


WIDE = False


def mx_kscale(k):
    if not WIDE:
        return np.ones(k)
    levels = np.array([10, -10, 5, -5, 0])
    if k % 512:
        return np.exp2(np.random.permutation(np.resize(levels, k // 32))).repeat(32)
    a = np.empty((k // 512, 16))
    for p in range(k // 512):
        a[p, :8] = np.random.permutation(np.resize(levels, 8))
        for g in range(8):
            far = levels[np.abs(levels - a[p, g]) >= 10]
            a[p, g + 8] = far[np.random.randint(len(far))]
    return np.exp2(a.ravel()).repeat(32)


BF16 = ml_dtypes.bfloat16


def bf(x):
    return np.asarray(x, np.float32).astype(BF16)


def f64(x):
    return np.asarray(x).astype(np.float64)


B_, S, D_IN, D_OUT, N, RANK, ALPHA = 4, 128, 2048, 2048, 32, 16, 32
NR = N * RANK
SCALE = ALPHA / RANK


def setup_inputs():
    s, t = mx_kscale(D_IN), mx_kscale(NR)
    tn = t.reshape(N, RANK)
    return {"x": bf(np.random.standard_normal((B_, S, D_IN)) * s),
            "lora_A": bf(np.random.standard_normal((N, RANK, D_IN)) / np.sqrt(D_IN) / s * tn[:, :, None]),
            "lora_B": bf(np.random.standard_normal((N, D_OUT, RANK)) / np.sqrt(RANK) / tn[:, None, :]),
            "W": bf(np.random.standard_normal((D_OUT, D_IN)) / np.sqrt(D_IN) / s),
            "bias": bf(np.random.standard_normal(D_OUT) * 0.3),
            "lora_weights": bf((1.0 + 0.5 * np.random.standard_normal(N)) * 2.0 / N)}


def reference(x, lora_A, lora_B, W, bias, lora_weights):
    xq = mxq(f64(x), 2, "e4m3")
    h = xq @ mxq(f64(lora_A).reshape(NR, D_IN), 1, "e4m3").T
    coef = (SCALE * f64(lora_weights))[:, None, None]
    bc = (f64(lora_B) * coef).transpose(1, 0, 2).reshape(D_OUT, NR)
    lora_out = mxq(h, 2, "e4m3") @ mxq(bc, 1, "e4m3").T
    base = (xq @ mxq(f64(W), 1, "e4m3").T) + f64(bias)
    return base + lora_out

@@ -1,0 +1,276 @@
+from contextlib import ExitStack
+
+import concourse.mybir as mybir
+from concourse.masks import make_identity
+
+F32 = mybir.dt.float32
+BF16 = mybir.dt.bfloat16
+U32 = mybir.dt.uint32
+U8 = mybir.dt.uint8
+FP8X4 = mybir.dt.float8_e4m3fn_x4
+ADD = mybir.AluOpType.add
+MULT = mybir.AluOpType.mult
+COPY = mybir.ActivationFunctionType.Copy
+
+P = 128
+TOK = 512
+D = 2048
+O = 2048
+NR = 512
+SCALE = 2.0
+FLOPS = 2 * TOK * D * O + 2 * TOK * D * NR + 2 * TOK * NR * O
+
+
+def tile_replaced_compose_lora_pa_kernel(tc, x, lora_A, lora_B, W, bias, lora_weights, out):
+    nc = tc.nc
+    with ExitStack() as ctx:
+        const = ctx.enter_context(tc.tile_pool(name="const", bufs=1))
+        raw = ctx.enter_context(tc.tile_pool(name="raw", bufs=4))
+        bpool = ctx.enter_context(tc.tile_pool(name="bpool", bufs=2))
+        grp = ctx.enter_context(tc.tile_pool(name="grp", bufs=3))
+        outp = ctx.enter_context(tc.tile_pool(name="outp", bufs=6))
+        tps = ctx.enter_context(tc.psum_pool(name="tps", bufs=4))
+        accp = ctx.enter_context(tc.psum_pool(name="accp", bufs=4))
+        ctx.enter_context(tc.manual_schedule())
+
+        x_rows = x.rearrange("b s d -> (b s) d")
+        a_rows = lora_A.rearrange("n r d -> (n r) d").rearrange("(q t) d -> q (t d)", t=4)
+        b_rows = lora_B.rearrange("n (p l) r -> p n (l r)", l=16)
+        w_rows = W.rearrange("(a p) d -> p a d", p=P)
+        out_rows = out.rearrange("b s o -> (b s) o")
+
+        ident = const.tile([P, P], F32, name="ident")
+        make_identity(nc, ident[:])
+
+        xq = const.tile([P, 2048], U32, name="xq", align_bytes=64)
+        xs = const.tile([P, 2048], U8, name="xs", align_bytes=64)
+        aq = const.tile([P, 2048], U32, name="aq", align_bytes=64)
+        asc = const.tile([P, 2048], U8, name="asc", align_bytes=64)
+        wq = const.tile([P, 8192], U32, name="wq", align_bytes=64)
+        ws = const.tile([P, 8192], U8, name="ws", align_bytes=64)
+        bq = const.tile([P, 2048], U32, name="bq", align_bytes=64)
+        bs = const.tile([P, 2048], U8, name="bs", align_bytes=64)
+        hq = const.tile([P, 512], U32, name="hq", align_bytes=64)
+        hs = const.tile([P, 512], U8, name="hs", align_bytes=64)
+        hg = const.tile([P, 2048], BF16, name="hg", align_bytes=64)
+        bias_b = const.tile([P, O], BF16, name="bias_b")
+        lw_b = const.tile([P, 32], BF16, name="lw_b")
+        sel = const.tile([P, P], F32, name="sel")
+        coef1 = const.tile([P, 1], F32, name="coef1")
+        coef = const.tile([P, 1], F32, name="coef")
+
+        x_sb = raw.tile([P, 8192], BF16, tag="raw", name="x_sb")
+        for tt in range(4):
+            nc.sync.dma_start(out=x_sb[:, tt * D:(tt + 1) * D], in_=x_rows[tt * P:(tt + 1) * P, :])
+        nc.sync.dma_start(out=lw_b[:], in_=lora_weights.partition_broadcast(P))
+        a_sb = raw.tile([P, 8192], BF16, tag="raw", name="a_sb")
+        for half in range(2):
+            nc.sync.dma_start(out=a_sb[:, half * 4096:(half + 1) * 4096], in_=a_rows[:, half * 4096:(half + 1) * 4096])
+
+        w_sb = []
+
+        def load_w(g):
+            w_t = raw.tile([P, 8192], BF16, tag="raw", name="w_sb%d" % g)
+            for half in range(2):
+                nc.sync.dma_start(
+                    out=w_t[:, half * 4096:(half + 1) * 4096].rearrange("p (a d) -> p a d", a=2),
+                    in_=w_rows[:, 4 * g + 2 * half:4 * g + 2 * half + 2, :],
+                )
+            w_sb.append(w_t)
+
+        load_w(0)
+        b_sb = bpool.tile([P, 8192], BF16, tag="b", name="b_sb", align_bytes=64)
+        for half in range(2):
+            nc.sync.dma_start(
+                out=b_sb[:, half * 4096:(half + 1) * 4096].rearrange("p (n k) -> p n k", k=256),
+                in_=b_rows[:, half * 16:(half + 1) * 16, :],
+            )
+        load_w(1)
+        nc.sync.dma_start(out=bias_b[:], in_=bias.partition_broadcast(P))
+
+        def t_unit(words, first):
+            banks = []
+            for c in range(4):
+                bank = tps.tile([P, 512], F32, tag="tp", name="bank")
+                for u in range(2):
+                    for i in range(2):
+                        col = (first + i) * 1024 + c * 2 * P
+                        nc.tensor.transpose(bank[:, (2 * u + i) * P:(2 * u + i + 1) * P], words[:, col + u:col + 2 * P:2], ident[:])
+                banks.append(bank)
+            return banks
+
+        def c_unit(banks):
+            g_t = grp.tile([P, 4096], BF16, tag="grp", name="g_t", align_bytes=64)
+            g_w = g_t[:].bitcast(F32)
+            for c in range(4):
+                nc.scalar.copy(
+                    out=g_w[:, c * 512:(c + 1) * 512].rearrange("p (k u) -> p k u", u=2),
+                    in_=banks[c][:].rearrange("p (u k) -> p k u", u=2),
+                )
+            return g_t
+
+        for (src_t, codes, planes) in ((x_sb, xq, xs), (a_sb, aq, asc)):
+            words = src_t[:].bitcast(F32)
+            for pair in range(2):
+                g_t = c_unit(t_unit(words, 2 * pair))
+                nc.vector.quantize_mx(
+                    out=codes[:, pair * 1024:(pair + 1) * 1024].bitcast(FP8X4),
+                    scales=planes[:, pair * 1024:(pair + 1) * 1024],
+                    in_=g_t[:],
+                )
+        load_w(2)
+        load_w(3)
+
+        nc.vector.tensor_tensor(
+            out=sel[:].rearrange("p (n s) -> p n s", s=4),
+            in0=ident[:].rearrange("p (n s) -> p n s", s=4),
+            in1=lw_b[:].unsqueeze(2).to_broadcast([P, 32, 4]),
+            op=MULT,
+        )
+        nc.vector.tensor_reduce(out=coef1[:], in_=sel[:], axis=mybir.AxisListType.X, op=ADD)
+        nc.vector.tensor_scalar(out=coef[:], in0=coef1[:], scalar1=SCALE, scalar2=None, op0=MULT)
+
+        def w_t(k):
+            return t_unit(w_sb[k // 2][:].bitcast(F32), 2 * (k % 2))
+
+        def w_q(k, g_t):
+            for c in range(4):
+                o0 = (k // 2) * 2048 + c * 512 + (k % 2) * 256
+                nc.vector.quantize_mx(
+                    out=wq[:, o0:o0 + 256].bitcast(FP8X4),
+                    scales=ws[:, o0:o0 + 256],
+                    in_=g_t[:, c * 1024:(c + 1) * 1024],
+                )
+
+        def w_cq(k, banks):
+            w_q(k, c_unit(banks))
+
+        def base(g, tt):
+            acc = accp.tile([P, 512], F32, tag="acc", name="acc")
+            x0 = (tt // 2) * 1024 + (tt % 2) * P
+            for c in range(4):
+                nc.tensor.matmul_mx(
+                    out=acc[:],
+                    lhsT=xq[:, x0 + c * 256:x0 + c * 256 + P].bitcast(FP8X4),
+                    lhsT_scale=xs[:, x0 + c * 256:x0 + c * 256 + P],
+                    rhs=wq[:, g * 2048 + c * 512:g * 2048 + (c + 1) * 512].bitcast(FP8X4),
+                    rhs_scale=ws[:, g * 2048 + c * 512:g * 2048 + (c + 1) * 512],
+                    start=(c == 0),
+                    stop=False,
+                )
+            return acc
+
+        def lora(g, tt, acc):
+            nc.tensor.matmul_mx(
+                out=acc[:],
+                lhsT=hq[:, tt * P:(tt + 1) * P].bitcast(FP8X4),
+                lhsT_scale=hs[:, tt * P:(tt + 1) * P],
+                rhs=bq[:, g * 512:(g + 1) * 512].bitcast(FP8X4),
+                rhs_scale=bs[:, g * 512:(g + 1) * 512],
+                start=False,
+                stop=True,
+            )
+
+        def fin(g, tt, acc):
+            o_sb = outp.tile([P, 512], F32, tag="o", name="o_sb")
+            nc.vector.tensor_tensor(out=o_sb[:], in0=acc[:], in1=bias_b[:, g * 512:(g + 1) * 512], op=ADD)
+            nc.sync.dma_start(out=out_rows[tt * P:(tt + 1) * P, g * 512:(g + 1) * 512], in_=o_sb[:])
+
+        bl = bpool.tile([P, 8192], BF16, tag="b", name="bl", align_bytes=64)
+        b_w = b_sb[:].bitcast(F32).rearrange("p (n l s u) -> p l u n s", n=32, l=16, s=4, u=2)
+        bl_w = bl[:].bitcast(F32)
+        bl_v = bl_w.rearrange("p (l u n s) -> p l u n s", l=16, u=2, n=32, s=4)
+
+        def sort_b(half):
+            for u in range(2):
+                nc.vector.tensor_copy(
+                    out=bl_v[:, :, u, half * 16:(half + 1) * 16, :],
+                    in_=b_w[:, :, u, half * 16:(half + 1) * 16, :],
+                )
+
+        h_acc = []
+
+        def h_groups(tt, ts):
+            x0 = (tt // 2) * 1024 + (tt % 2) * P
+            for t in ts:
+                a0 = (t // 2) * 1024 + (t % 2) * P
+                for c in range(4):
+                    nc.tensor.matmul_mx(
+                        out=h_acc[tt][:, t * P:(t + 1) * P],
+                        lhsT=aq[:, a0 + c * 256:a0 + c * 256 + P].bitcast(FP8X4),
+                        lhsT_scale=asc[:, a0 + c * 256:a0 + c * 256 + P],
+                        rhs=xq[:, x0 + c * 256:x0 + c * 256 + P].bitcast(FP8X4),
+                        rhs_scale=xs[:, x0 + c * 256:x0 + c * 256 + P],
+                        start=(c == 0),
+                        stop=(c == 3),
+                    )
+
+        w_cq(0, w_t(0))
+        for tt in range(4):
+            acc = accp.tile([P, 512], F32, tag="acc", name="acc")
+            h_acc.append(acc)
+            h_groups(tt, (0, 1))
+        g_t = c_unit(w_t(1))
+        sort_b(0)
+        w_q(1, g_t)
+        for tt in range(4):
+            h_groups(tt, (2, 3))
+            nc.scalar.copy(
+                out=hg[:, tt * 512:(tt + 1) * 512].rearrange("q (r t) -> q r t", t=4),
+                in_=h_acc[tt][:].rearrange("q (t r) -> q r t", t=4),
+            )
+        sort_b(1)
+        nc.vector.quantize_mx(out=hq[:].bitcast(FP8X4), scales=hs[:], in_=hg[:])
+
+        accs = [base(0, 0), base(0, 1)]
+
+        bg = bpool.tile([P, 8192], BF16, tag="b", name="bg", align_bytes=64)
+        bg_v = bg[:].bitcast(F32).rearrange("q (p l a) -> q p l a", p=P, l=8, a=4)
+        for lp in range(8):
+            bank = tps.tile([P, 512], F32, tag="tp", name="bankb")
+            for a in range(4):
+                col = (2 * lp + a // 2) * 256 + (a % 2) * P
+                nc.tensor.transpose(bank[:, a * P:(a + 1) * P], bl_w[:, col:col + P], ident[:])
+            src = bank[:].rearrange("q (a p) -> q p a", a=4)
+            if (lp // 2) % 2 == 0:
+                nc.scalar.copy(out=bg_v[:, :, lp, :], in_=src)
+            else:
+                nc.vector.tensor_copy(out=bg_v[:, :, lp, :], in_=src)
+
+        def b_scale_quantise(half):
+            part = bg[:, half * 4096:(half + 1) * 4096]
+            nc.vector.tensor_scalar(out=part, in0=part, scalar1=coef[:, 0:1], scalar2=None, op0=MULT)
+            nc.vector.quantize_mx(
+                out=bq[:, half * 1024:(half + 1) * 1024].bitcast(FP8X4),
+                scales=bs[:, half * 1024:(half + 1) * 1024],
+                in_=part,
+            )
+
+        accs.append(base(0, 2))
+        banks = w_t(2)
+        b_scale_quantise(0)
+        w_cq(2, banks)
+        accs.append(base(0, 3))
+        w_cq(3, w_t(3))
+        for tt in range(4):
+            lora(0, tt, accs[tt])
+        banks = w_t(4)
+        fin(0, 0, accs[0])
+        fin(0, 1, accs[1])
+        w_cq(4, banks)
+        fin(0, 2, accs[2])
+        fin(0, 3, accs[3])
+        b_scale_quantise(1)
+
+        for m in range(2, 8):
+            g = m // 2
+            accs = []
+            for tt in (2 * (m % 2), 2 * (m % 2) + 1):
+                acc = base(g, tt)
+                lora(g, tt, acc)
+                accs.append(acc)
+            banks = w_t(m + 3) if m + 3 < 8 else None
+            fin(g, 2 * (m % 2), accs[0])
+            fin(g, 2 * (m % 2) + 1, accs[1])
+            if m + 3 < 8:
+                w_cq(m + 3, banks)

@@ -27,6 +27,7 @@ def tile_replaced_compose_lora_pa_kernel(tc, x, lora_A, lora_B, W, bias, lora_we
         const = ctx.enter_context(tc.tile_pool(name="const", bufs=1))
         raw = ctx.enter_context(tc.tile_pool(name="raw", bufs=4))
         bpool = ctx.enter_context(tc.tile_pool(name="bpool", bufs=2))
+        perm = ctx.enter_context(tc.tile_pool(name="perm", bufs=2))
         grp = ctx.enter_context(tc.tile_pool(name="grp", bufs=3))
         outp = ctx.enter_context(tc.tile_pool(name="outp", bufs=6))
         tps = ctx.enter_context(tc.psum_pool(name="tps", bufs=4))
@@ -88,14 +89,18 @@ def tile_replaced_compose_lora_pa_kernel(tc, x, lora_A, lora_B, W, bias, lora_we
         load_w(1)
         nc.sync.dma_start(out=bias_b[:], in_=bias.partition_broadcast(P))
 
-        def t_unit(words, first):
+        def t_unit(words, first, step=2):
             banks = []
             for c in range(4):
                 bank = tps.tile([P, 512], F32, tag="tp", name="bank")
                 for u in range(2):
                     for i in range(2):
                         col = (first + i) * 1024 + c * 2 * P
-                        nc.tensor.transpose(bank[:, (2 * u + i) * P:(2 * u + i + 1) * P], words[:, col + u:col + 2 * P:2], ident[:])
+                        if step == 2:
+                            src = words[:, col + u:col + 2 * P:2]
+                        else:
+                            src = words[:, col + u * P:col + (u + 1) * P]
+                        nc.tensor.transpose(bank[:, (2 * u + i) * P:(2 * u + i + 1) * P], src, ident[:])
                 banks.append(bank)
             return banks
 
@@ -109,10 +114,22 @@ def tile_replaced_compose_lora_pa_kernel(tc, x, lora_A, lora_B, W, bias, lora_we
                 )
             return g_t
 
+        w_perm = {}
+
+        def w_p(k):
+            p_t = perm.tile([P, 4096], BF16, tag="perm", name="p_t")
+            nc.vector.tensor_copy(
+                out=p_t[:].bitcast(F32).rearrange("p (g u j) -> p g u j", u=2, j=P),
+                in_=w_sb[k // 2][:, (k % 2) * 4096:(k % 2 + 1) * 4096].bitcast(F32).rearrange("p (g j u) -> p g u j", u=2, j=P),
+            )
+            w_perm[k] = p_t
+
         for (src_t, codes, planes) in ((x_sb, xq, xs), (a_sb, aq, asc)):
             words = src_t[:].bitcast(F32)
             for pair in range(2):
                 g_t = c_unit(t_unit(words, 2 * pair))
+                if src_t is a_sb and pair == 1:
+                    w_p(0)
                 nc.vector.quantize_mx(
                     out=codes[:, pair * 1024:(pair + 1) * 1024].bitcast(FP8X4),
                     scales=planes[:, pair * 1024:(pair + 1) * 1024],
@@ -120,7 +137,6 @@ def tile_replaced_compose_lora_pa_kernel(tc, x, lora_A, lora_B, W, bias, lora_we
                 )
         load_w(2)
         load_w(3)
-
         nc.vector.tensor_tensor(
             out=sel[:].rearrange("p (n s) -> p n s", s=4),
             in0=ident[:].rearrange("p (n s) -> p n s", s=4),
@@ -131,7 +147,7 @@ def tile_replaced_compose_lora_pa_kernel(tc, x, lora_A, lora_B, W, bias, lora_we
         nc.vector.tensor_scalar(out=coef[:], in0=coef1[:], scalar1=SCALE, scalar2=None, op0=MULT)
 
         def w_t(k):
-            return t_unit(w_sb[k // 2][:].bitcast(F32), 2 * (k % 2))
+            return t_unit(w_perm[k][:].bitcast(F32), 0, 1)
 
         def w_q(k, g_t):
             for c in range(4):
@@ -205,6 +221,7 @@ def tile_replaced_compose_lora_pa_kernel(tc, x, lora_A, lora_B, W, bias, lora_we
                         stop=(c == 3),
                     )
 
+        w_p(1)
         w_cq(0, w_t(0))
         for tt in range(4):
             acc = accp.tile([P, 512], F32, tag="acc", name="acc")
@@ -220,6 +237,7 @@ def tile_replaced_compose_lora_pa_kernel(tc, x, lora_A, lora_B, W, bias, lora_we
                 in_=h_acc[tt][:].rearrange("q (t r) -> q r t", t=4),
             )
         sort_b(1)
+        w_p(2)
         nc.vector.quantize_mx(out=hq[:].bitcast(FP8X4), scales=hs[:], in_=hg[:])
 
         accs = [base(0, 0), base(0, 1)]
@@ -248,10 +266,13 @@ def tile_replaced_compose_lora_pa_kernel(tc, x, lora_A, lora_B, W, bias, lora_we
 
         accs.append(base(0, 2))
         banks = w_t(2)
+        w_p(3)
         b_scale_quantise(0)
         w_cq(2, banks)
+        w_p(4)
         accs.append(base(0, 3))
         w_cq(3, w_t(3))
+        w_p(5)
         for tt in range(4):
             lora(0, tt, accs[tt])
         banks = w_t(4)
@@ -264,6 +285,8 @@ def tile_replaced_compose_lora_pa_kernel(tc, x, lora_A, lora_B, W, bias, lora_we
 
         for m in range(2, 8):
             g = m // 2
+            if m + 4 < 8:
+                w_p(m + 4)
             accs = []
             for tt in (2 * (m % 2), 2 * (m % 2) + 1):
                 acc = base(g, tt)

@@ -63,7 +63,6 @@ def tile_replaced_compose_lora_pa_kernel(tc, x, lora_A, lora_B, W, bias, lora_we
         x_sb = raw.tile([P, 8192], BF16, tag="raw", name="x_sb")
         for tt in range(4):
             nc.sync.dma_start(out=x_sb[:, tt * D:(tt + 1) * D], in_=x_rows[tt * P:(tt + 1) * P, :])
-        nc.sync.dma_start(out=lw_b[:], in_=lora_weights.partition_broadcast(P))
         a_sb = raw.tile([P, 8192], BF16, tag="raw", name="a_sb")
         for half in range(2):
             nc.sync.dma_start(out=a_sb[:, half * 4096:(half + 1) * 4096], in_=a_rows[:, half * 4096:(half + 1) * 4096])
@@ -86,8 +85,8 @@ def tile_replaced_compose_lora_pa_kernel(tc, x, lora_A, lora_B, W, bias, lora_we
                 out=b_sb[:, half * 4096:(half + 1) * 4096].rearrange("p (n k) -> p n k", k=256),
                 in_=b_rows[:, half * 16:(half + 1) * 16, :],
             )
+        nc.sync.dma_start(out=lw_b[:], in_=lora_weights.partition_broadcast(P))
         load_w(1)
-        nc.sync.dma_start(out=bias_b[:], in_=bias.partition_broadcast(P))
 
         def t_unit(words, first, step=2):
             banks = []
@@ -137,15 +136,7 @@ def tile_replaced_compose_lora_pa_kernel(tc, x, lora_A, lora_B, W, bias, lora_we
                 )
         load_w(2)
         load_w(3)
-        nc.vector.tensor_tensor(
-            out=sel[:].rearrange("p (n s) -> p n s", s=4),
-            in0=ident[:].rearrange("p (n s) -> p n s", s=4),
-            in1=lw_b[:].unsqueeze(2).to_broadcast([P, 32, 4]),
-            op=MULT,
-        )
-        nc.vector.tensor_reduce(out=coef1[:], in_=sel[:], axis=mybir.AxisListType.X, op=ADD)
-        nc.vector.tensor_scalar(out=coef[:], in0=coef1[:], scalar1=SCALE, scalar2=None, op0=MULT)
-
+        nc.sync.dma_start(out=bias_b[:], in_=bias.partition_broadcast(P))
         def w_t(k):
             return t_unit(w_perm[k][:].bitcast(F32), 0, 1)
 
@@ -239,6 +230,15 @@ def tile_replaced_compose_lora_pa_kernel(tc, x, lora_A, lora_B, W, bias, lora_we
         sort_b(1)
         w_p(2)
         nc.vector.quantize_mx(out=hq[:].bitcast(FP8X4), scales=hs[:], in_=hg[:])
+
+        nc.vector.tensor_tensor(
+            out=sel[:].rearrange("p (n s) -> p n s", s=4),
+            in0=ident[:].rearrange("p (n s) -> p n s", s=4),
+            in1=lw_b[:].unsqueeze(2).to_broadcast([P, 32, 4]),
+            op=MULT,
+        )
+        nc.vector.tensor_reduce(out=coef1[:], in_=sel[:], axis=mybir.AxisListType.X, op=ADD)
+        nc.vector.tensor_scalar(out=coef[:], in0=coef1[:], scalar1=SCALE, scalar2=None, op0=MULT)
 
         accs = [base(0, 0), base(0, 1)]
 

@@ -27,9 +27,9 @@ def tile_replaced_compose_lora_pa_kernel(tc, x, lora_A, lora_B, W, bias, lora_we
         const = ctx.enter_context(tc.tile_pool(name="const", bufs=1))
         raw = ctx.enter_context(tc.tile_pool(name="raw", bufs=4))
         bpool = ctx.enter_context(tc.tile_pool(name="bpool", bufs=2))
-        perm = ctx.enter_context(tc.tile_pool(name="perm", bufs=2))
+        perm = ctx.enter_context(tc.tile_pool(name="perm", bufs=3))
         grp = ctx.enter_context(tc.tile_pool(name="grp", bufs=3))
-        outp = ctx.enter_context(tc.tile_pool(name="outp", bufs=6))
+        outp = ctx.enter_context(tc.tile_pool(name="outp", bufs=4))
         tps = ctx.enter_context(tc.psum_pool(name="tps", bufs=4))
         accp = ctx.enter_context(tc.psum_pool(name="accp", bufs=4))
         ctx.enter_context(tc.manual_schedule())
@@ -64,8 +64,8 @@ def tile_replaced_compose_lora_pa_kernel(tc, x, lora_A, lora_B, W, bias, lora_we
         for tt in range(4):
             nc.sync.dma_start(out=x_sb[:, tt * D:(tt + 1) * D], in_=x_rows[tt * P:(tt + 1) * P, :])
         a_sb = raw.tile([P, 8192], BF16, tag="raw", name="a_sb")
-        for half in range(2):
-            nc.sync.dma_start(out=a_sb[:, half * 4096:(half + 1) * 4096], in_=a_rows[:, half * 4096:(half + 1) * 4096])
+        for t in range(4):
+            nc.sync.dma_start(out=a_sb[:, t * D:(t + 1) * D], in_=a_rows[:, t * D:(t + 1) * D])
 
         w_sb = []
 
@@ -78,7 +78,6 @@ def tile_replaced_compose_lora_pa_kernel(tc, x, lora_A, lora_B, W, bias, lora_we
                 )
             w_sb.append(w_t)
 
-        load_w(0)
         b_sb = bpool.tile([P, 8192], BF16, tag="b", name="b_sb", align_bytes=64)
         for half in range(2):
             nc.sync.dma_start(
@@ -86,20 +85,52 @@ def tile_replaced_compose_lora_pa_kernel(tc, x, lora_A, lora_B, W, bias, lora_we
                 in_=b_rows[:, half * 16:(half + 1) * 16, :],
             )
         nc.sync.dma_start(out=lw_b[:], in_=lora_weights.partition_broadcast(P))
+        load_w(0)
         load_w(1)
+        nc.sync.dma_start(out=bias_b[:], in_=bias.partition_broadcast(P))
 
-        def t_unit(words, first, step=2):
+        def t_row(p_t):
+            words = p_t[:].bitcast(F32)
+            banks = []
+            for h in range(2):
+                bank = tps.tile([P, 512], F32, tag="tp", name="bank")
+                for j in range(4):
+                    col = (4 * h + j) * P
+                    nc.tensor.transpose(bank[:, j * P:(j + 1) * P], words[:, col:col + P], ident[:])
+                banks.append(bank)
+            return banks
+
+        def c_row(banks):
+            g_t = grp.tile([P, 2048], BF16, tag="grp", name="gx_t", align_bytes=64)
+            g_w = g_t[:].bitcast(F32)
+            for h in range(2):
+                nc.scalar.copy(
+                    out=g_w[:, h * 512:(h + 1) * 512].rearrange("p (c k u) -> p c k u", c=2, u=2),
+                    in_=banks[h][:].rearrange("p (c u k) -> p c k u", c=2, u=2),
+                )
+            return g_t
+
+        def q_row(codes, planes, r, g_t):
+            nc.vector.quantize_mx(
+                out=codes[:, r * 512:(r + 1) * 512].bitcast(FP8X4),
+                scales=planes[:, r * 512:(r + 1) * 512],
+                in_=g_t[:],
+            )
+
+        def p_row(src_t, r):
+            p_t = perm.tile([P, 2048], BF16, tag="perm", name="px_t")
+            permute(nc.vector.tensor_copy, p_t[:], src_t[:, r * D:(r + 1) * D])
+            return p_t
+
+        def t_unit_w(p_t):
+            words = p_t[:].bitcast(F32)
             banks = []
             for c in range(4):
                 bank = tps.tile([P, 512], F32, tag="tp", name="bank")
                 for u in range(2):
                     for i in range(2):
-                        col = (first + i) * 1024 + c * 2 * P
-                        if step == 2:
-                            src = words[:, col + u:col + 2 * P:2]
-                        else:
-                            src = words[:, col + u * P:col + (u + 1) * P]
-                        nc.tensor.transpose(bank[:, (2 * u + i) * P:(2 * u + i + 1) * P], src, ident[:])
+                        col = i * 1024 + c * 256 + u * P
+                        nc.tensor.transpose(bank[:, (2 * u + i) * P:(2 * u + i + 1) * P], words[:, col:col + P], ident[:])
                 banks.append(bank)
             return banks
 
@@ -113,32 +144,23 @@ def tile_replaced_compose_lora_pa_kernel(tc, x, lora_A, lora_B, W, bias, lora_we
                 )
             return g_t
 
+        def permute(copy, dst, src):
+            copy(
+                out=dst.bitcast(F32).rearrange("p (g u b w) -> p g u b w", u=2, b=16, w=8),
+                in_=src.bitcast(F32).rearrange("p (g b u w) -> p g u b w", u=2, b=16, w=8),
+            )
+
         w_perm = {}
 
-        def w_p(k):
+        def w_p(k, engines="vv"):
             p_t = perm.tile([P, 4096], BF16, tag="perm", name="p_t")
-            nc.vector.tensor_copy(
-                out=p_t[:].bitcast(F32).rearrange("p (g u j) -> p g u j", u=2, j=P),
-                in_=w_sb[k // 2][:, (k % 2) * 4096:(k % 2 + 1) * 4096].bitcast(F32).rearrange("p (g j u) -> p g u j", u=2, j=P),
-            )
+            for i in range(2):
+                copy = nc.scalar.copy if engines[i] == "s" else nc.vector.tensor_copy
+                permute(copy, p_t[:, i * D:(i + 1) * D], w_sb[k // 2][:, (k % 2) * 4096 + i * D:(k % 2) * 4096 + (i + 1) * D])
             w_perm[k] = p_t
 
-        for (src_t, codes, planes) in ((x_sb, xq, xs), (a_sb, aq, asc)):
-            words = src_t[:].bitcast(F32)
-            for pair in range(2):
-                g_t = c_unit(t_unit(words, 2 * pair))
-                if src_t is a_sb and pair == 1:
-                    w_p(0)
-                nc.vector.quantize_mx(
-                    out=codes[:, pair * 1024:(pair + 1) * 1024].bitcast(FP8X4),
-                    scales=planes[:, pair * 1024:(pair + 1) * 1024],
-                    in_=g_t[:],
-                )
-        load_w(2)
-        load_w(3)
-        nc.sync.dma_start(out=bias_b[:], in_=bias.partition_broadcast(P))
         def w_t(k):
-            return t_unit(w_perm[k][:].bitcast(F32), 0, 1)
+            return t_unit_w(w_perm[k])
 
         def w_q(k, g_t):
             for c in range(4):
@@ -154,12 +176,12 @@ def tile_replaced_compose_lora_pa_kernel(tc, x, lora_A, lora_B, W, bias, lora_we
 
         def base(g, tt):
             acc = accp.tile([P, 512], F32, tag="acc", name="acc")
-            x0 = (tt // 2) * 1024 + (tt % 2) * P
+            x0 = tt * 512
             for c in range(4):
                 nc.tensor.matmul_mx(
                     out=acc[:],
-                    lhsT=xq[:, x0 + c * 256:x0 + c * 256 + P].bitcast(FP8X4),
-                    lhsT_scale=xs[:, x0 + c * 256:x0 + c * 256 + P],
+                    lhsT=xq[:, x0 + c * P:x0 + (c + 1) * P].bitcast(FP8X4),
+                    lhsT_scale=xs[:, x0 + c * P:x0 + (c + 1) * P],
                     rhs=wq[:, g * 2048 + c * 512:g * 2048 + (c + 1) * 512].bitcast(FP8X4),
                     rhs_scale=ws[:, g * 2048 + c * 512:g * 2048 + (c + 1) * 512],
                     start=(c == 0),
@@ -188,112 +210,131 @@ def tile_replaced_compose_lora_pa_kernel(tc, x, lora_A, lora_B, W, bias, lora_we
         bl_w = bl[:].bitcast(F32)
         bl_v = bl_w.rearrange("p (l u n s) -> p l u n s", l=16, u=2, n=32, s=4)
 
-        def sort_b(half):
+        def sort_b(half, engines="vv"):
             for u in range(2):
-                nc.vector.tensor_copy(
-                    out=bl_v[:, :, u, half * 16:(half + 1) * 16, :],
-                    in_=b_w[:, :, u, half * 16:(half + 1) * 16, :],
-                )
+                dst = bl_v[:, :, u, half * 16:(half + 1) * 16, :]
+                src = b_w[:, :, u, half * 16:(half + 1) * 16, :]
+                if engines[u] == "v":
+                    nc.vector.tensor_copy(out=dst, in_=src)
+                else:
+                    nc.scalar.copy(out=dst, in_=src)
 
         h_acc = []
 
         def h_groups(tt, ts):
-            x0 = (tt // 2) * 1024 + (tt % 2) * P
+            x0 = tt * 512
             for t in ts:
-                a0 = (t // 2) * 1024 + (t % 2) * P
+                a0 = t * 512
                 for c in range(4):
                     nc.tensor.matmul_mx(
                         out=h_acc[tt][:, t * P:(t + 1) * P],
-                        lhsT=aq[:, a0 + c * 256:a0 + c * 256 + P].bitcast(FP8X4),
-                        lhsT_scale=asc[:, a0 + c * 256:a0 + c * 256 + P],
-                        rhs=xq[:, x0 + c * 256:x0 + c * 256 + P].bitcast(FP8X4),
-                        rhs_scale=xs[:, x0 + c * 256:x0 + c * 256 + P],
+                        lhsT=aq[:, a0 + c * P:a0 + (c + 1) * P].bitcast(FP8X4),
+                        lhsT_scale=asc[:, a0 + c * P:a0 + (c + 1) * P],
+                        rhs=xq[:, x0 + c * P:x0 + (c + 1) * P].bitcast(FP8X4),
+                        rhs_scale=xs[:, x0 + c * P:x0 + (c + 1) * P],
                         start=(c == 0),
                         stop=(c == 3),
                     )
 
-        w_p(1)
-        w_cq(0, w_t(0))
-        for tt in range(4):
-            acc = accp.tile([P, 512], F32, tag="acc", name="acc")
-            h_acc.append(acc)
-            h_groups(tt, (0, 1))
-        g_t = c_unit(w_t(1))
-        sort_b(0)
-        w_q(1, g_t)
-        for tt in range(4):
-            h_groups(tt, (2, 3))
+        def h_copy(tt):
             nc.scalar.copy(
                 out=hg[:, tt * 512:(tt + 1) * 512].rearrange("q (r t) -> q r t", t=4),
                 in_=h_acc[tt][:].rearrange("q (t r) -> q r t", t=4),
             )
-        sort_b(1)
-        w_p(2)
-        nc.vector.quantize_mx(out=hq[:].bitcast(FP8X4), scales=hs[:], in_=hg[:])
 
-        nc.vector.tensor_tensor(
-            out=sel[:].rearrange("p (n s) -> p n s", s=4),
-            in0=ident[:].rearrange("p (n s) -> p n s", s=4),
-            in1=lw_b[:].unsqueeze(2).to_broadcast([P, 32, 4]),
-            op=MULT,
-        )
-        nc.vector.tensor_reduce(out=coef1[:], in_=sel[:], axis=mybir.AxisListType.X, op=ADD)
-        nc.vector.tensor_scalar(out=coef[:], in0=coef1[:], scalar1=SCALE, scalar2=None, op0=MULT)
-
-        accs = [base(0, 0), base(0, 1)]
+        def coefficients():
+            nc.vector.tensor_tensor(
+                out=sel[:].rearrange("p (n s) -> p n s", s=4),
+                in0=ident[:].rearrange("p (n s) -> p n s", s=4),
+                in1=lw_b[:].unsqueeze(2).to_broadcast([P, 32, 4]),
+                op=MULT,
+            )
+            nc.vector.tensor_reduce(out=coef1[:], in_=sel[:], axis=mybir.AxisListType.X, op=ADD)
+            nc.vector.tensor_scalar(out=coef[:], in0=coef1[:], scalar1=SCALE, scalar2=None, op0=MULT)
 
         bg = bpool.tile([P, 8192], BF16, tag="b", name="bg", align_bytes=64)
         bg_v = bg[:].bitcast(F32).rearrange("q (p l a) -> q p l a", p=P, l=8, a=4)
-        for lp in range(8):
+
+        def b_t(lp, engine):
             bank = tps.tile([P, 512], F32, tag="tp", name="bankb")
             for a in range(4):
                 col = (2 * lp + a // 2) * 256 + (a % 2) * P
                 nc.tensor.transpose(bank[:, a * P:(a + 1) * P], bl_w[:, col:col + P], ident[:])
             src = bank[:].rearrange("q (a p) -> q p a", a=4)
-            if (lp // 2) % 2 == 0:
+            if engine == "s":
                 nc.scalar.copy(out=bg_v[:, :, lp, :], in_=src)
             else:
                 nc.vector.tensor_copy(out=bg_v[:, :, lp, :], in_=src)
 
-        def b_scale_quantise(half):
+        def b_scale(half):
             part = bg[:, half * 4096:(half + 1) * 4096]
             nc.vector.tensor_scalar(out=part, in0=part, scalar1=coef[:, 0:1], scalar2=None, op0=MULT)
+
+        def b_quant(half):
             nc.vector.quantize_mx(
                 out=bq[:, half * 1024:(half + 1) * 1024].bitcast(FP8X4),
                 scales=bs[:, half * 1024:(half + 1) * 1024],
-                in_=part,
+                in_=bg[:, half * 4096:(half + 1) * 4096],
             )
 
-        accs.append(base(0, 2))
-        banks = w_t(2)
-        w_p(3)
-        b_scale_quantise(0)
-        w_cq(2, banks)
-        w_p(4)
-        accs.append(base(0, 3))
-        w_cq(3, w_t(3))
-        w_p(5)
+        rows = [(x_sb, xq, xs, r) for r in range(4)] + [(a_sb, aq, asc, r) for r in range(4)]
+        groups = []
+        for n in range(8):
+            src_t, codes, planes, r = rows[n]
+            groups.append(c_row(t_row(p_row(src_t, r))))
+            if n >= 2:
+                q_row(rows[n - 2][1], rows[n - 2][2], rows[n - 2][3], groups[n - 2])
+        load_w(2)
+        load_w(3)
+        q_row(aq, asc, 2, groups[6])
+        q_row(aq, asc, 3, groups[7])
         for tt in range(4):
-            lora(0, tt, accs[tt])
-        banks = w_t(4)
-        fin(0, 0, accs[0])
-        fin(0, 1, accs[1])
-        w_cq(4, banks)
-        fin(0, 2, accs[2])
-        fin(0, 3, accs[3])
-        b_scale_quantise(1)
+            acc = accp.tile([P, 512], F32, tag="acc", name="acc")
+            h_acc.append(acc)
+            h_groups(tt, (0, 1))
+        for tt in range(2):
+            h_groups(tt, (2, 3))
+        sort_b(0, "vs")
+        sort_b(1, "vs")
+        coefficients()
+        w_p(0)
+        for lp in range(4):
+            b_t(lp, "sv"[lp // 2])
+        h_copy(0)
+        h_copy(1)
+        for tt in range(2, 4):
+            h_groups(tt, (2, 3))
+            h_copy(tt)
+        w_p(1)
+        for lp in range(4, 8):
+            b_t(lp, "sv"[lp // 2 - 2])
+        nc.vector.quantize_mx(out=hq[:].bitcast(FP8X4), scales=hs[:], in_=hg[:])
+        g_w = c_unit(w_t(0))
+        w_p(2)
+        w_q(0, g_w)
+        g_w = c_unit(w_t(1))
+        b_scale(0)
+        w_q(1, g_w)
+        g_w = c_unit(w_t(2))
+        b_quant(0)
+        w_p(3)
+        w_q(2, g_w)
 
-        for m in range(2, 8):
+        for m in range(8):
             g = m // 2
             if m + 4 < 8:
-                w_p(m + 4)
+                w_p(m + 4, "vv")
             accs = []
             for tt in (2 * (m % 2), 2 * (m % 2) + 1):
                 acc = base(g, tt)
                 lora(g, tt, acc)
                 accs.append(acc)
             banks = w_t(m + 3) if m + 3 < 8 else None
+            if m == 0:
+                b_scale(1)
             fin(g, 2 * (m % 2), accs[0])
             fin(g, 2 * (m % 2) + 1, accs[1])
             if m + 3 < 8:
                 w_cq(m + 3, banks)
+            if m == 0:
+                b_quant(1)

@@ -27,7 +27,7 @@ def tile_replaced_compose_lora_pa_kernel(tc, x, lora_A, lora_B, W, bias, lora_we
         const = ctx.enter_context(tc.tile_pool(name="const", bufs=1))
         raw = ctx.enter_context(tc.tile_pool(name="raw", bufs=4))
         bpool = ctx.enter_context(tc.tile_pool(name="bpool", bufs=2))
-        perm = ctx.enter_context(tc.tile_pool(name="perm", bufs=3))
+        perm = ctx.enter_context(tc.tile_pool(name="perm", bufs=2))
         grp = ctx.enter_context(tc.tile_pool(name="grp", bufs=3))
         outp = ctx.enter_context(tc.tile_pool(name="outp", bufs=4))
         tps = ctx.enter_context(tc.psum_pool(name="tps", bufs=4))
@@ -66,7 +66,6 @@ def tile_replaced_compose_lora_pa_kernel(tc, x, lora_A, lora_B, W, bias, lora_we
         a_sb = raw.tile([P, 8192], BF16, tag="raw", name="a_sb")
         for t in range(4):
             nc.sync.dma_start(out=a_sb[:, t * D:(t + 1) * D], in_=a_rows[:, t * D:(t + 1) * D])
-
         w_sb = []
 
         def load_w(g):
@@ -78,6 +77,7 @@ def tile_replaced_compose_lora_pa_kernel(tc, x, lora_A, lora_B, W, bias, lora_we
                 )
             w_sb.append(w_t)
 
+        load_w(0)
         b_sb = bpool.tile([P, 8192], BF16, tag="b", name="b_sb", align_bytes=64)
         for half in range(2):
             nc.sync.dma_start(
@@ -85,18 +85,17 @@ def tile_replaced_compose_lora_pa_kernel(tc, x, lora_A, lora_B, W, bias, lora_we
                 in_=b_rows[:, half * 16:(half + 1) * 16, :],
             )
         nc.sync.dma_start(out=lw_b[:], in_=lora_weights.partition_broadcast(P))
-        load_w(0)
         load_w(1)
         nc.sync.dma_start(out=bias_b[:], in_=bias.partition_broadcast(P))
 
-        def t_row(p_t):
-            words = p_t[:].bitcast(F32)
+        def t_row(src_t, r):
+            words = src_t[:].bitcast(F32)
             banks = []
             for h in range(2):
                 bank = tps.tile([P, 512], F32, tag="tp", name="bank")
                 for j in range(4):
-                    col = (4 * h + j) * P
-                    nc.tensor.transpose(bank[:, j * P:(j + 1) * P], words[:, col:col + P], ident[:])
+                    col = r * 1024 + (2 * h + j // 2) * 256 + j % 2
+                    nc.tensor.transpose(bank[:, j * P:(j + 1) * P], words[:, col:col + 255:2], ident[:])
                 banks.append(bank)
             return banks
 
@@ -110,6 +109,14 @@ def tile_replaced_compose_lora_pa_kernel(tc, x, lora_A, lora_B, W, bias, lora_we
                 )
             return g_t
 
+        def c_half(g_t, i, banks):
+            g_v = g_t[:].bitcast(F32).rearrange("p (c i k u) -> p i c k u", c=4, i=2, u=2)
+            for h in range(2):
+                nc.scalar.copy(
+                    out=g_v[:, i, 2 * h:2 * h + 2],
+                    in_=banks[h][:].rearrange("p (c u k) -> p c k u", c=2, u=2),
+                )
+
         def q_row(codes, planes, r, g_t):
             nc.vector.quantize_mx(
                 out=codes[:, r * 512:(r + 1) * 512].bitcast(FP8X4),
@@ -117,13 +124,43 @@ def tile_replaced_compose_lora_pa_kernel(tc, x, lora_A, lora_B, W, bias, lora_we
                 in_=g_t[:],
             )
 
-        def p_row(src_t, r):
-            p_t = perm.tile([P, 2048], BF16, tag="perm", name="px_t")
-            permute(nc.vector.tensor_copy, p_t[:], src_t[:, r * D:(r + 1) * D])
-            return p_t
+        def q_pair(pair, g_t):
+            nc.vector.quantize_mx(
+                out=xq[:, pair * 1024:(pair + 1) * 1024].bitcast(FP8X4),
+                scales=xs[:, pair * 1024:(pair + 1) * 1024],
+                in_=g_t[:],
+            )
 
-        def t_unit_w(p_t):
-            words = p_t[:].bitcast(F32)
+        def g_tile():
+            return grp.tile([P, 4096], BF16, tag="grp", name="g_t", align_bytes=64)
+
+        def c_unit(banks, engines="ssss", g_t=None, cs=(0, 1, 2, 3)):
+            if g_t is None:
+                g_t = g_tile()
+            g_w = g_t[:].bitcast(F32)
+            for n, c in enumerate(cs):
+                dst = g_w[:, c * 512:(c + 1) * 512].rearrange("p (k u) -> p k u", u=2)
+                src = banks[n][:].rearrange("p (u k) -> p k u", u=2)
+                if engines[n] == "s":
+                    nc.scalar.copy(out=dst, in_=src)
+                else:
+                    nc.vector.tensor_copy(out=dst, in_=src)
+            return g_t
+
+        def w_p(k, engines):
+            p_t = perm.tile([P, 4096], BF16, tag="perm", name="p_t")
+            for i in range(2):
+                copy = nc.scalar.copy if engines[i] == "s" else nc.vector.tensor_copy
+                copy(
+                    out=p_t[:, i * D:(i + 1) * D].bitcast(F32).rearrange("p (c u j) -> p c u j", c=4, u=2),
+                    in_=w_sb[k // 2][:, (2 * (k % 2) + i) * D:(2 * (k % 2) + i + 1) * D].bitcast(F32).rearrange("p (c j u) -> p c u j", c=4, u=2),
+                )
+            w_perm[k] = p_t
+
+        w_perm = {}
+
+        def w_t(k):
+            words = w_perm[k][:].bitcast(F32)
             banks = []
             for c in range(4):
                 bank = tps.tile([P, 512], F32, tag="tp", name="bank")
@@ -134,36 +171,8 @@ def tile_replaced_compose_lora_pa_kernel(tc, x, lora_A, lora_B, W, bias, lora_we
                 banks.append(bank)
             return banks
 
-        def c_unit(banks):
-            g_t = grp.tile([P, 4096], BF16, tag="grp", name="g_t", align_bytes=64)
-            g_w = g_t[:].bitcast(F32)
-            for c in range(4):
-                nc.scalar.copy(
-                    out=g_w[:, c * 512:(c + 1) * 512].rearrange("p (k u) -> p k u", u=2),
-                    in_=banks[c][:].rearrange("p (u k) -> p k u", u=2),
-                )
-            return g_t
-
-        def permute(copy, dst, src):
-            copy(
-                out=dst.bitcast(F32).rearrange("p (g u b w) -> p g u b w", u=2, b=16, w=8),
-                in_=src.bitcast(F32).rearrange("p (g b u w) -> p g u b w", u=2, b=16, w=8),
-            )
-
-        w_perm = {}
-
-        def w_p(k, engines="vv"):
-            p_t = perm.tile([P, 4096], BF16, tag="perm", name="p_t")
-            for i in range(2):
-                copy = nc.scalar.copy if engines[i] == "s" else nc.vector.tensor_copy
-                permute(copy, p_t[:, i * D:(i + 1) * D], w_sb[k // 2][:, (k % 2) * 4096 + i * D:(k % 2) * 4096 + (i + 1) * D])
-            w_perm[k] = p_t
-
-        def w_t(k):
-            return t_unit_w(w_perm[k])
-
-        def w_q(k, g_t):
-            for c in range(4):
+        def w_q(k, g_t, cs=(0, 1, 2, 3)):
+            for c in cs:
                 o0 = (k // 2) * 2048 + c * 512 + (k % 2) * 256
                 nc.vector.quantize_mx(
                     out=wq[:, o0:o0 + 256].bitcast(FP8X4),
@@ -171,17 +180,14 @@ def tile_replaced_compose_lora_pa_kernel(tc, x, lora_A, lora_B, W, bias, lora_we
                     in_=g_t[:, c * 1024:(c + 1) * 1024],
                 )
 
-        def w_cq(k, banks):
-            w_q(k, c_unit(banks))
-
         def base(g, tt):
             acc = accp.tile([P, 512], F32, tag="acc", name="acc")
-            x0 = tt * 512
             for c in range(4):
+                x0 = (tt // 2) * 1024 + c * 256 + (tt % 2) * P
                 nc.tensor.matmul_mx(
                     out=acc[:],
-                    lhsT=xq[:, x0 + c * P:x0 + (c + 1) * P].bitcast(FP8X4),
-                    lhsT_scale=xs[:, x0 + c * P:x0 + (c + 1) * P],
+                    lhsT=xq[:, x0:x0 + P].bitcast(FP8X4),
+                    lhsT_scale=xs[:, x0:x0 + P],
                     rhs=wq[:, g * 2048 + c * 512:g * 2048 + (c + 1) * 512].bitcast(FP8X4),
                     rhs_scale=ws[:, g * 2048 + c * 512:g * 2048 + (c + 1) * 512],
                     start=(c == 0),
@@ -199,6 +205,35 @@ def tile_replaced_compose_lora_pa_kernel(tc, x, lora_A, lora_B, W, bias, lora_we
                 start=False,
                 stop=True,
             )
+
+        def last_tile(g, tt):
+            for half in range(2):
+                acc = accp.tile([P, 256], F32, tag="acc", name="acc")
+                o0 = half * 256
+                for c in range(4):
+                    x0 = (tt // 2) * 1024 + c * 256 + (tt % 2) * P
+                    w0 = g * 2048 + c * 512 + o0
+                    nc.tensor.matmul_mx(
+                        out=acc[:],
+                        lhsT=xq[:, x0:x0 + P].bitcast(FP8X4),
+                        lhsT_scale=xs[:, x0:x0 + P],
+                        rhs=wq[:, w0:w0 + 256].bitcast(FP8X4),
+                        rhs_scale=ws[:, w0:w0 + 256],
+                        start=(c == 0),
+                        stop=False,
+                    )
+                nc.tensor.matmul_mx(
+                    out=acc[:],
+                    lhsT=hq[:, tt * P:(tt + 1) * P].bitcast(FP8X4),
+                    lhsT_scale=hs[:, tt * P:(tt + 1) * P],
+                    rhs=bq[:, g * 512 + o0:g * 512 + o0 + 256].bitcast(FP8X4),
+                    rhs_scale=bs[:, g * 512 + o0:g * 512 + o0 + 256],
+                    start=False,
+                    stop=True,
+                )
+                o_sb = outp.tile([P, 256], F32, tag="o", name="o_sb")
+                nc.vector.tensor_tensor(out=o_sb[:], in0=acc[:], in1=bias_b[:, g * 512 + o0:g * 512 + o0 + 256], op=ADD)
+                nc.sync.dma_start(out=out_rows[tt * P:(tt + 1) * P, g * 512 + o0:g * 512 + o0 + 256], in_=o_sb[:])
 
         def fin(g, tt, acc):
             o_sb = outp.tile([P, 512], F32, tag="o", name="o_sb")
@@ -219,27 +254,29 @@ def tile_replaced_compose_lora_pa_kernel(tc, x, lora_A, lora_B, W, bias, lora_we
                 else:
                     nc.scalar.copy(out=dst, in_=src)
 
-        h_acc = []
+        h_acc = {}
 
-        def h_groups(tt, ts):
-            x0 = tt * 512
-            for t in ts:
-                a0 = t * 512
+        def h_groups(pair, tp):
+            acc = accp.tile([P, 512], F32, tag="acc", name="acc")
+            for i in range(2):
+                a0 = (2 * tp + i) * 512
                 for c in range(4):
+                    x0 = pair * 1024 + c * 256
                     nc.tensor.matmul_mx(
-                        out=h_acc[tt][:, t * P:(t + 1) * P],
+                        out=acc[:, i * 256:(i + 1) * 256],
                         lhsT=aq[:, a0 + c * P:a0 + (c + 1) * P].bitcast(FP8X4),
                         lhsT_scale=asc[:, a0 + c * P:a0 + (c + 1) * P],
-                        rhs=xq[:, x0 + c * P:x0 + (c + 1) * P].bitcast(FP8X4),
-                        rhs_scale=xs[:, x0 + c * P:x0 + (c + 1) * P],
+                        rhs=xq[:, x0:x0 + 256].bitcast(FP8X4),
+                        rhs_scale=xs[:, x0:x0 + 256],
                         start=(c == 0),
                         stop=(c == 3),
                     )
+            h_acc[pair, tp] = acc
 
-        def h_copy(tt):
+        def h_copy(pair, tp):
             nc.scalar.copy(
-                out=hg[:, tt * 512:(tt + 1) * 512].rearrange("q (r t) -> q r t", t=4),
-                in_=h_acc[tt][:].rearrange("q (t r) -> q r t", t=4),
+                out=hg[:].rearrange("q (r t) -> q r t", t=4)[:, pair * 256:(pair + 1) * 256, 2 * tp:2 * tp + 2],
+                in_=h_acc[pair, tp][:].rearrange("q (t r) -> q r t", t=2),
             )
 
         def coefficients():
@@ -277,64 +314,84 @@ def tile_replaced_compose_lora_pa_kernel(tc, x, lora_A, lora_B, W, bias, lora_we
                 in_=bg[:, half * 4096:(half + 1) * 4096],
             )
 
-        rows = [(x_sb, xq, xs, r) for r in range(4)] + [(a_sb, aq, asc, r) for r in range(4)]
-        groups = []
-        for n in range(8):
-            src_t, codes, planes, r = rows[n]
-            groups.append(c_row(t_row(p_row(src_t, r))))
-            if n >= 2:
-                q_row(rows[n - 2][1], rows[n - 2][2], rows[n - 2][3], groups[n - 2])
+        gx = []
+        for pair in range(2):
+            g_t = g_tile()
+            for i in range(2):
+                c_half(g_t, i, t_row(x_sb, 2 * pair + i))
+            gx.append(g_t)
+            if pair == 1:
+                q_pair(0, gx[0])
+        ga = []
+        for r in range(4):
+            ga.append(c_row(t_row(a_sb, r)))
+            if r == 0:
+                q_pair(1, gx[1])
+            else:
+                q_row(aq, asc, r - 1, ga[r - 1])
         load_w(2)
         load_w(3)
-        q_row(aq, asc, 2, groups[6])
-        q_row(aq, asc, 3, groups[7])
-        for tt in range(4):
-            acc = accp.tile([P, 512], F32, tag="acc", name="acc")
-            h_acc.append(acc)
-            h_groups(tt, (0, 1))
-        for tt in range(2):
-            h_groups(tt, (2, 3))
+        q_row(aq, asc, 3, ga[3])
+        w_p(0, "vv")
+        h_groups(0, 0)
+        h_groups(1, 0)
+        h_copy(0, 0)
+        h_copy(1, 0)
+        g_w = c_unit(w_t(0))
+        w_p(1, "vv")
+        w_q(0, g_w)
+        h_groups(0, 1)
+        h_copy(0, 1)
+        g_w = c_unit(w_t(1))
+        h_groups(1, 1)
+        h_copy(1, 1)
+        w_q(1, g_w)
         sort_b(0, "vs")
         sort_b(1, "vs")
         coefficients()
-        w_p(0)
+        nc.vector.quantize_mx(out=hq[:].bitcast(FP8X4), scales=hs[:], in_=hg[:])
+        w_p(2, "sv")
+        accs = [base(0, 0), base(0, 1)]
         for lp in range(4):
             b_t(lp, "sv"[lp // 2])
-        h_copy(0)
-        h_copy(1)
-        for tt in range(2, 4):
-            h_groups(tt, (2, 3))
-            h_copy(tt)
-        w_p(1)
+        accs.append(base(0, 2))
         for lp in range(4, 8):
             b_t(lp, "sv"[lp // 2 - 2])
-        nc.vector.quantize_mx(out=hq[:].bitcast(FP8X4), scales=hs[:], in_=hg[:])
-        g_w = c_unit(w_t(0))
-        w_p(2)
-        w_q(0, g_w)
-        g_w = c_unit(w_t(1))
+        w_p(3, "ss")
+        accs.append(base(0, 3))
         b_scale(0)
-        w_q(1, g_w)
-        g_w = c_unit(w_t(2))
+        g_w = c_unit(w_t(2), "svsv")
         b_quant(0)
-        w_p(3)
         w_q(2, g_w)
-
-        for m in range(8):
+        w_p(4, "sv")
+        g_w = c_unit(w_t(3))
+        for tt in range(4):
+            lora(0, tt, accs[tt])
+        fin(0, 0, accs[0])
+        w_q(3, g_w)
+        fin(0, 1, accs[1])
+        w_p(5, "sv")
+        g_w = c_unit(w_t(4))
+        for tt in range(2, 4):
+            fin(0, tt, accs[tt])
+        w_q(4, g_w)
+        b_scale(1)
+        for m in range(2, 8):
             g = m // 2
-            if m + 4 < 8:
-                w_p(m + 4, "vv")
+            tts = (2 * (m % 2), 2 * (m % 2) + 1)
+            k = m + 3
+            if k + 1 < 8:
+                w_p(k + 1, "sv")
             accs = []
-            for tt in (2 * (m % 2), 2 * (m % 2) + 1):
-                acc = base(g, tt)
-                lora(g, tt, acc)
-                accs.append(acc)
-            banks = w_t(m + 3) if m + 3 < 8 else None
-            if m == 0:
-                b_scale(1)
-            fin(g, 2 * (m % 2), accs[0])
-            fin(g, 2 * (m % 2) + 1, accs[1])
-            if m + 3 < 8:
-                w_cq(m + 3, banks)
-            if m == 0:
+            for tt in tts if m < 7 else tts[:1]:
+                accs.append(base(g, tt))
+                lora(g, tt, accs[-1])
+            if k < 8:
+                g_w = c_unit(w_t(k))
+            for j in range(len(accs)):
+                fin(g, tts[j], accs[j])
+            if m == 2:
                 b_quant(1)
+            if k < 8:
+                w_q(k, g_w)
+        last_tile(3, 3)

@@ -347,20 +347,20 @@ def tile_replaced_compose_lora_pa_kernel(tc, x, lora_A, lora_B, W, bias, lora_we
         h_copy(1, 1)
         w_q(1, g_w)
         sort_b(0, "vs")
-        sort_b(1, "vs")
+        sort_b(1)
         coefficients()
         nc.vector.quantize_mx(out=hq[:].bitcast(FP8X4), scales=hs[:], in_=hg[:])
         w_p(2, "sv")
         accs = [base(0, 0), base(0, 1)]
         for lp in range(4):
             b_t(lp, "sv"[lp // 2])
+        w_p(3, "sv")
         accs.append(base(0, 2))
         for lp in range(4, 8):
             b_t(lp, "sv"[lp // 2 - 2])
-        w_p(3, "ss")
         accs.append(base(0, 3))
         b_scale(0)
-        g_w = c_unit(w_t(2), "svsv")
+        g_w = c_unit(w_t(2))
         b_quant(0)
         w_q(2, g_w)
         w_p(4, "sv")

@@ -159,10 +159,10 @@ def tile_replaced_compose_lora_pa_kernel(tc, x, lora_A, lora_B, W, bias, lora_we
 
         w_perm = {}
 
-        def w_t(k):
+        def w_t(k, cs=(0, 1, 2, 3)):
             words = w_perm[k][:].bitcast(F32)
             banks = []
-            for c in range(4):
+            for c in cs:
                 bank = tps.tile([P, 512], F32, tag="tp", name="bank")
                 for u in range(2):
                     for i in range(2):
@@ -378,20 +378,22 @@ def tile_replaced_compose_lora_pa_kernel(tc, x, lora_A, lora_B, W, bias, lora_we
         b_scale(1)
         for m in range(2, 8):
             g = m // 2
-            tts = (2 * (m % 2), 2 * (m % 2) + 1)
             k = m + 3
             if k + 1 < 8:
                 w_p(k + 1, "sv")
-            accs = []
-            for tt in tts if m < 7 else tts[:1]:
-                accs.append(base(g, tt))
-                lora(g, tt, accs[-1])
-            if k < 8:
-                g_w = c_unit(w_t(k))
-            for j in range(len(accs)):
-                fin(g, tts[j], accs[j])
-            if m == 2:
-                b_quant(1)
-            if k < 8:
-                w_q(k, g_w)
-        last_tile(3, 3)
+            g_w = g_tile() if k < 8 else None
+            for j in range(2):
+                tt = 2 * (m % 2) + j
+                if (m, j) == (7, 1):
+                    last_tile(g, tt)
+                    continue
+                acc = base(g, tt)
+                lora(g, tt, acc)
+                cs = (2 * j, 2 * j + 1)
+                if k < 8:
+                    c_unit(w_t(k, cs), "ss", g_w, cs)
+                fin(g, tt, acc)
+                if (m, j) == (2, 1):
+                    b_quant(1)
+                if k < 8:
+                    w_q(k, g_w, cs)

@@ -64,9 +64,13 @@ def tile_replaced_compose_lora_pa_kernel(tc, x, lora_A, lora_B, W, bias, lora_we
         for tt in range(4):
             nc.sync.dma_start(out=x_sb[:, tt * D:(tt + 1) * D], in_=x_rows[tt * P:(tt + 1) * P, :])
         a_sb = raw.tile([P, 8192], BF16, tag="raw", name="a_sb")
-        for t in range(4):
-            nc.sync.dma_start(out=a_sb[:, t * D:(t + 1) * D], in_=a_rows[:, t * D:(t + 1) * D])
+        for t0, t1 in ((0, 1), (1, 2), (2, 3), (3, 3.5), (3.5, 4)):
+            cols = slice(int(t0 * D), int(t1 * D))
+            nc.sync.dma_start(out=a_sb[:, cols], in_=a_rows[:, cols])
         w_sb = []
+
+        def load_bias():
+            nc.sync.dma_start(out=bias_b[:], in_=bias.partition_broadcast(P))
 
         def load_w(g):
             w_t = raw.tile([P, 8192], BF16, tag="raw", name="w_sb%d" % g)
@@ -75,6 +79,8 @@ def tile_replaced_compose_lora_pa_kernel(tc, x, lora_A, lora_B, W, bias, lora_we
                     out=w_t[:, half * 4096:(half + 1) * 4096].rearrange("p (a d) -> p a d", a=2),
                     in_=w_rows[:, 4 * g + 2 * half:4 * g + 2 * half + 2, :],
                 )
+                if (g, half) == (2, 0):
+                    load_bias()
             w_sb.append(w_t)
 
         load_w(0)
@@ -86,7 +92,6 @@ def tile_replaced_compose_lora_pa_kernel(tc, x, lora_A, lora_B, W, bias, lora_we
             )
         nc.sync.dma_start(out=lw_b[:], in_=lora_weights.partition_broadcast(P))
         load_w(1)
-        nc.sync.dma_start(out=bias_b[:], in_=bias.partition_broadcast(P))
 
         def t_row(src_t, r):
             words = src_t[:].bitcast(F32)
@@ -350,15 +355,15 @@ def tile_replaced_compose_lora_pa_kernel(tc, x, lora_A, lora_B, W, bias, lora_we
         sort_b(1)
         coefficients()
         nc.vector.quantize_mx(out=hq[:].bitcast(FP8X4), scales=hs[:], in_=hg[:])
-        w_p(2, "sv")
         accs = [base(0, 0), base(0, 1)]
-        for lp in range(4):
+        for lp in range(0, 4):
             b_t(lp, "sv"[lp // 2])
-        w_p(3, "sv")
         accs.append(base(0, 2))
+        w_p(2, "sv")
         for lp in range(4, 8):
             b_t(lp, "sv"[lp // 2 - 2])
         accs.append(base(0, 3))
+        w_p(3, "sv")
         b_scale(0)
         g_w = c_unit(w_t(2))
         b_quant(0)
@@ -370,7 +375,7 @@ def tile_replaced_compose_lora_pa_kernel(tc, x, lora_A, lora_B, W, bias, lora_we
         fin(0, 0, accs[0])
         w_q(3, g_w)
         fin(0, 1, accs[1])
-        w_p(5, "sv")
+        w_p(5, "vv")
         g_w = c_unit(w_t(4))
         for tt in range(2, 4):
             fin(0, tt, accs[tt])

@@ -185,9 +185,10 @@ def tile_replaced_compose_lora_pa_kernel(tc, x, lora_A, lora_B, W, bias, lora_we
                     in_=g_t[:, c * 1024:(c + 1) * 1024],
                 )
 
-        def base(g, tt):
-            acc = accp.tile([P, 512], F32, tag="acc", name="acc")
-            for c in range(4):
+        def base(g, tt, acc=None, cs=(0, 1, 2, 3)):
+            if acc is None:
+                acc = accp.tile([P, 512], F32, tag="acc", name="acc")
+            for c in cs:
                 x0 = (tt // 2) * 1024 + c * 256 + (tt % 2) * P
                 nc.tensor.matmul_mx(
                     out=acc[:],
@@ -356,27 +357,32 @@ def tile_replaced_compose_lora_pa_kernel(tc, x, lora_A, lora_B, W, bias, lora_we
         coefficients()
         nc.vector.quantize_mx(out=hq[:].bitcast(FP8X4), scales=hs[:], in_=hg[:])
         accs = [base(0, 0), base(0, 1)]
-        for lp in range(0, 4):
+        for lp in range(4):
             b_t(lp, "sv"[lp // 2])
         accs.append(base(0, 2))
         w_p(2, "sv")
         for lp in range(4, 8):
             b_t(lp, "sv"[lp // 2 - 2])
-        accs.append(base(0, 3))
+        accs.append(base(0, 3, cs=(0, 1)))
         w_p(3, "sv")
         b_scale(0)
         g_w = c_unit(w_t(2))
+        base(0, 3, accs[3], (2, 3))
         b_quant(0)
         w_q(2, g_w)
         w_p(4, "sv")
         g_w = c_unit(w_t(3))
-        for tt in range(4):
-            lora(0, tt, accs[tt])
+        lora(0, 0, accs[0])
+        lora(0, 1, accs[1])
         fin(0, 0, accs[0])
         w_q(3, g_w)
         fin(0, 1, accs[1])
         w_p(5, "vv")
-        g_w = c_unit(w_t(4))
+        g_w = g_tile()
+        c_unit(w_t(4, (0, 1)), "ss", g_w, (0, 1))
+        lora(0, 2, accs[2])
+        lora(0, 3, accs[3])
+        c_unit(w_t(4, (2, 3)), "ss", g_w, (2, 3))
         for tt in range(2, 4):
             fin(0, tt, accs[tt])
         w_q(4, g_w)

from contextlib import ExitStack

import concourse.mybir as mybir
from concourse.masks import make_identity

F32 = mybir.dt.float32
BF16 = mybir.dt.bfloat16
U32 = mybir.dt.uint32
U8 = mybir.dt.uint8
FP8X4 = mybir.dt.float8_e4m3fn_x4
ADD = mybir.AluOpType.add
MULT = mybir.AluOpType.mult
COPY = mybir.ActivationFunctionType.Copy

P = 128
TOK = 512
D = 2048
O = 2048
NR = 512
SCALE = 2.0
FLOPS = 2 * TOK * D * O + 2 * TOK * D * NR + 2 * TOK * NR * O


def tile_replaced_compose_lora_pa_kernel(tc, x, lora_A, lora_B, W, bias, lora_weights, out):
    nc = tc.nc
    with ExitStack() as ctx:
        const = ctx.enter_context(tc.tile_pool(name="const", bufs=1))
        raw = ctx.enter_context(tc.tile_pool(name="raw", bufs=4))
        bpool = ctx.enter_context(tc.tile_pool(name="bpool", bufs=2))
        perm = ctx.enter_context(tc.tile_pool(name="perm", bufs=2))
        grp = ctx.enter_context(tc.tile_pool(name="grp", bufs=3))
        outp = ctx.enter_context(tc.tile_pool(name="outp", bufs=4))
        tps = ctx.enter_context(tc.psum_pool(name="tps", bufs=4))
        accp = ctx.enter_context(tc.psum_pool(name="accp", bufs=4))
        ctx.enter_context(tc.manual_schedule())

        x_rows = x.rearrange("b s d -> (b s) d")
        a_rows = lora_A.rearrange("n r d -> (n r) d").rearrange("(q t) d -> q (t d)", t=4)
        b_rows = lora_B.rearrange("n (p l) r -> p n (l r)", l=16)
        w_rows = W.rearrange("(a p) d -> p a d", p=P)
        out_rows = out.rearrange("b s o -> (b s) o")

        ident = const.tile([P, P], F32, name="ident")
        make_identity(nc, ident[:])

        xq = const.tile([P, 2048], U32, name="xq", align_bytes=64)
        xs = const.tile([P, 2048], U8, name="xs", align_bytes=64)
        aq = const.tile([P, 2048], U32, name="aq", align_bytes=64)
        asc = const.tile([P, 2048], U8, name="asc", align_bytes=64)
        wq = const.tile([P, 8192], U32, name="wq", align_bytes=64)
        ws = const.tile([P, 8192], U8, name="ws", align_bytes=64)
        bq = const.tile([P, 2048], U32, name="bq", align_bytes=64)
        bs = const.tile([P, 2048], U8, name="bs", align_bytes=64)
        hq = const.tile([P, 512], U32, name="hq", align_bytes=64)
        hs = const.tile([P, 512], U8, name="hs", align_bytes=64)
        hg = const.tile([P, 2048], BF16, name="hg", align_bytes=64)
        bias_b = const.tile([P, O], BF16, name="bias_b")
        lw_b = const.tile([P, 32], BF16, name="lw_b")
        sel = const.tile([P, P], F32, name="sel")
        coef1 = const.tile([P, 1], F32, name="coef1")
        coef = const.tile([P, 1], F32, name="coef")

        x_sb = raw.tile([P, 8192], BF16, tag="raw", name="x_sb")
        for tt in range(4):
            nc.sync.dma_start(out=x_sb[:, tt * D:(tt + 1) * D], in_=x_rows[tt * P:(tt + 1) * P, :])
        a_sb = raw.tile([P, 8192], BF16, tag="raw", name="a_sb")
        for t0, t1 in ((0, 1), (1, 2), (2, 3), (3, 3.5), (3.5, 4)):
            cols = slice(int(t0 * D), int(t1 * D))
            nc.sync.dma_start(out=a_sb[:, cols], in_=a_rows[:, cols])
        w_sb = []

        def load_bias():
            nc.sync.dma_start(out=bias_b[:], in_=bias.partition_broadcast(P))

        def load_w(g):
            w_t = raw.tile([P, 8192], BF16, tag="raw", name="w_sb%d" % g)
            for half in range(2):
                nc.sync.dma_start(
                    out=w_t[:, half * 4096:(half + 1) * 4096].rearrange("p (a d) -> p a d", a=2),
                    in_=w_rows[:, 4 * g + 2 * half:4 * g + 2 * half + 2, :],
                )
                if (g, half) == (2, 0):
                    load_bias()
            w_sb.append(w_t)

        load_w(0)
        b_sb = bpool.tile([P, 8192], BF16, tag="b", name="b_sb", align_bytes=64)
        for half in range(2):
            nc.sync.dma_start(
                out=b_sb[:, half * 4096:(half + 1) * 4096].rearrange("p (n k) -> p n k", k=256),
                in_=b_rows[:, half * 16:(half + 1) * 16, :],
            )
        nc.sync.dma_start(out=lw_b[:], in_=lora_weights.partition_broadcast(P))
        load_w(1)

        def t_row(src_t, r):
            words = src_t[:].bitcast(F32)
            banks = []
            for h in range(2):
                bank = tps.tile([P, 512], F32, tag="tp", name="bank")
                for j in range(4):
                    col = r * 1024 + (2 * h + j // 2) * 256 + j % 2
                    nc.tensor.transpose(bank[:, j * P:(j + 1) * P], words[:, col:col + 255:2], ident[:])
                banks.append(bank)
            return banks

        def c_row(banks):
            g_t = grp.tile([P, 2048], BF16, tag="grp", name="gx_t", align_bytes=64)
            g_w = g_t[:].bitcast(F32)
            for h in range(2):
                nc.scalar.copy(
                    out=g_w[:, h * 512:(h + 1) * 512].rearrange("p (c k u) -> p c k u", c=2, u=2),
                    in_=banks[h][:].rearrange("p (c u k) -> p c k u", c=2, u=2),
                )
            return g_t

        def c_half(g_t, i, banks):
            g_v = g_t[:].bitcast(F32).rearrange("p (c i k u) -> p i c k u", c=4, i=2, u=2)
            for h in range(2):
                nc.scalar.copy(
                    out=g_v[:, i, 2 * h:2 * h + 2],
                    in_=banks[h][:].rearrange("p (c u k) -> p c k u", c=2, u=2),
                )

        def q_row(codes, planes, r, g_t):
            nc.vector.quantize_mx(
                out=codes[:, r * 512:(r + 1) * 512].bitcast(FP8X4),
                scales=planes[:, r * 512:(r + 1) * 512],
                in_=g_t[:],
            )

        def q_pair(pair, g_t):
            nc.vector.quantize_mx(
                out=xq[:, pair * 1024:(pair + 1) * 1024].bitcast(FP8X4),
                scales=xs[:, pair * 1024:(pair + 1) * 1024],
                in_=g_t[:],
            )

        def g_tile():
            return grp.tile([P, 4096], BF16, tag="grp", name="g_t", align_bytes=64)

        def c_unit(banks, engines="ssss", g_t=None, cs=(0, 1, 2, 3)):
            if g_t is None:
                g_t = g_tile()
            g_w = g_t[:].bitcast(F32)
            for n, c in enumerate(cs):
                dst = g_w[:, c * 512:(c + 1) * 512].rearrange("p (k u) -> p k u", u=2)
                src = banks[n][:].rearrange("p (u k) -> p k u", u=2)
                if engines[n] == "s":
                    nc.scalar.copy(out=dst, in_=src)
                else:
                    nc.vector.tensor_copy(out=dst, in_=src)
            return g_t

        def w_p(k, engines):
            p_t = perm.tile([P, 4096], BF16, tag="perm", name="p_t")
            for i in range(2):
                copy = nc.scalar.copy if engines[i] == "s" else nc.vector.tensor_copy
                copy(
                    out=p_t[:, i * D:(i + 1) * D].bitcast(F32).rearrange("p (c u j) -> p c u j", c=4, u=2),
                    in_=w_sb[k // 2][:, (2 * (k % 2) + i) * D:(2 * (k % 2) + i + 1) * D].bitcast(F32).rearrange("p (c j u) -> p c u j", c=4, u=2),
                )
            w_perm[k] = p_t

        w_perm = {}

        def w_t(k, cs=(0, 1, 2, 3)):
            words = w_perm[k][:].bitcast(F32)
            banks = []
            for c in cs:
                bank = tps.tile([P, 512], F32, tag="tp", name="bank")
                for u in range(2):
                    for i in range(2):
                        col = i * 1024 + c * 256 + u * P
                        nc.tensor.transpose(bank[:, (2 * u + i) * P:(2 * u + i + 1) * P], words[:, col:col + P], ident[:])
                banks.append(bank)
            return banks

        def w_q(k, g_t, cs=(0, 1, 2, 3)):
            for c in cs:
                o0 = (k // 2) * 2048 + c * 512 + (k % 2) * 256
                nc.vector.quantize_mx(
                    out=wq[:, o0:o0 + 256].bitcast(FP8X4),
                    scales=ws[:, o0:o0 + 256],
                    in_=g_t[:, c * 1024:(c + 1) * 1024],
                )

        def base(g, tt, acc=None, cs=(0, 1, 2, 3)):
            if acc is None:
                acc = accp.tile([P, 512], F32, tag="acc", name="acc")
            for c in cs:
                x0 = (tt // 2) * 1024 + c * 256 + (tt % 2) * P
                nc.tensor.matmul_mx(
                    out=acc[:],
                    lhsT=xq[:, x0:x0 + P].bitcast(FP8X4),
                    lhsT_scale=xs[:, x0:x0 + P],
                    rhs=wq[:, g * 2048 + c * 512:g * 2048 + (c + 1) * 512].bitcast(FP8X4),
                    rhs_scale=ws[:, g * 2048 + c * 512:g * 2048 + (c + 1) * 512],
                    start=(c == 0),
                    stop=False,
                )
            return acc

        def lora(g, tt, acc):
            nc.tensor.matmul_mx(
                out=acc[:],
                lhsT=hq[:, tt * P:(tt + 1) * P].bitcast(FP8X4),
                lhsT_scale=hs[:, tt * P:(tt + 1) * P],
                rhs=bq[:, g * 512:(g + 1) * 512].bitcast(FP8X4),
                rhs_scale=bs[:, g * 512:(g + 1) * 512],
                start=False,
                stop=True,
            )

        def last_tile(g, tt):
            for half in range(2):
                acc = accp.tile([P, 256], F32, tag="acc", name="acc")
                o0 = half * 256
                for c in range(4):
                    x0 = (tt // 2) * 1024 + c * 256 + (tt % 2) * P
                    w0 = g * 2048 + c * 512 + o0
                    nc.tensor.matmul_mx(
                        out=acc[:],
                        lhsT=xq[:, x0:x0 + P].bitcast(FP8X4),
                        lhsT_scale=xs[:, x0:x0 + P],
                        rhs=wq[:, w0:w0 + 256].bitcast(FP8X4),
                        rhs_scale=ws[:, w0:w0 + 256],
                        start=(c == 0),
                        stop=False,
                    )
                nc.tensor.matmul_mx(
                    out=acc[:],
                    lhsT=hq[:, tt * P:(tt + 1) * P].bitcast(FP8X4),
                    lhsT_scale=hs[:, tt * P:(tt + 1) * P],
                    rhs=bq[:, g * 512 + o0:g * 512 + o0 + 256].bitcast(FP8X4),
                    rhs_scale=bs[:, g * 512 + o0:g * 512 + o0 + 256],
                    start=False,
                    stop=True,
                )
                o_sb = outp.tile([P, 256], F32, tag="o", name="o_sb")
                nc.vector.tensor_tensor(out=o_sb[:], in0=acc[:], in1=bias_b[:, g * 512 + o0:g * 512 + o0 + 256], op=ADD)
                nc.sync.dma_start(out=out_rows[tt * P:(tt + 1) * P, g * 512 + o0:g * 512 + o0 + 256], in_=o_sb[:])

        def fin(g, tt, acc):
            o_sb = outp.tile([P, 512], F32, tag="o", name="o_sb")
            nc.vector.tensor_tensor(out=o_sb[:], in0=acc[:], in1=bias_b[:, g * 512:(g + 1) * 512], op=ADD)
            nc.sync.dma_start(out=out_rows[tt * P:(tt + 1) * P, g * 512:(g + 1) * 512], in_=o_sb[:])

        bl = bpool.tile([P, 8192], BF16, tag="b", name="bl", align_bytes=64)
        b_w = b_sb[:].bitcast(F32).rearrange("p (n l s u) -> p l u n s", n=32, l=16, s=4, u=2)
        bl_w = bl[:].bitcast(F32)
        bl_v = bl_w.rearrange("p (l u n s) -> p l u n s", l=16, u=2, n=32, s=4)

        def sort_b(half, engines="vv"):
            for u in range(2):
                dst = bl_v[:, :, u, half * 16:(half + 1) * 16, :]
                src = b_w[:, :, u, half * 16:(half + 1) * 16, :]
                if engines[u] == "v":
                    nc.vector.tensor_copy(out=dst, in_=src)
                else:
                    nc.scalar.copy(out=dst, in_=src)

        h_acc = {}

        def h_groups(pair, tp):
            acc = accp.tile([P, 512], F32, tag="acc", name="acc")
            for i in range(2):
                a0 = (2 * tp + i) * 512
                for c in range(4):
                    x0 = pair * 1024 + c * 256
                    nc.tensor.matmul_mx(
                        out=acc[:, i * 256:(i + 1) * 256],
                        lhsT=aq[:, a0 + c * P:a0 + (c + 1) * P].bitcast(FP8X4),
                        lhsT_scale=asc[:, a0 + c * P:a0 + (c + 1) * P],
                        rhs=xq[:, x0:x0 + 256].bitcast(FP8X4),
                        rhs_scale=xs[:, x0:x0 + 256],
                        start=(c == 0),
                        stop=(c == 3),
                    )
            h_acc[pair, tp] = acc

        def h_copy(pair, tp):
            nc.scalar.copy(
                out=hg[:].rearrange("q (r t) -> q r t", t=4)[:, pair * 256:(pair + 1) * 256, 2 * tp:2 * tp + 2],
                in_=h_acc[pair, tp][:].rearrange("q (t r) -> q r t", t=2),
            )

        def coefficients():
            nc.vector.tensor_tensor(
                out=sel[:].rearrange("p (n s) -> p n s", s=4),
                in0=ident[:].rearrange("p (n s) -> p n s", s=4),
                in1=lw_b[:].unsqueeze(2).to_broadcast([P, 32, 4]),
                op=MULT,
            )
            nc.vector.tensor_reduce(out=coef1[:], in_=sel[:], axis=mybir.AxisListType.X, op=ADD)
            nc.vector.tensor_scalar(out=coef[:], in0=coef1[:], scalar1=SCALE, scalar2=None, op0=MULT)

        bg = bpool.tile([P, 8192], BF16, tag="b", name="bg", align_bytes=64)
        bg_v = bg[:].bitcast(F32).rearrange("q (p l a) -> q p l a", p=P, l=8, a=4)

        def b_t(lp, engine):
            bank = tps.tile([P, 512], F32, tag="tp", name="bankb")
            for a in range(4):
                col = (2 * lp + a // 2) * 256 + (a % 2) * P
                nc.tensor.transpose(bank[:, a * P:(a + 1) * P], bl_w[:, col:col + P], ident[:])
            src = bank[:].rearrange("q (a p) -> q p a", a=4)
            if engine == "s":
                nc.scalar.copy(out=bg_v[:, :, lp, :], in_=src)
            else:
                nc.vector.tensor_copy(out=bg_v[:, :, lp, :], in_=src)

        def b_scale(half):
            part = bg[:, half * 4096:(half + 1) * 4096]
            nc.vector.tensor_scalar(out=part, in0=part, scalar1=coef[:, 0:1], scalar2=None, op0=MULT)

        def b_quant(half):
            nc.vector.quantize_mx(
                out=bq[:, half * 1024:(half + 1) * 1024].bitcast(FP8X4),
                scales=bs[:, half * 1024:(half + 1) * 1024],
                in_=bg[:, half * 4096:(half + 1) * 4096],
            )

        gx = []
        for pair in range(2):
            g_t = g_tile()
            for i in range(2):
                c_half(g_t, i, t_row(x_sb, 2 * pair + i))
            gx.append(g_t)
            if pair == 1:
                q_pair(0, gx[0])
        ga = []
        for r in range(4):
            ga.append(c_row(t_row(a_sb, r)))
            if r == 0:
                q_pair(1, gx[1])
            else:
                q_row(aq, asc, r - 1, ga[r - 1])
        load_w(2)
        load_w(3)
        q_row(aq, asc, 3, ga[3])
        w_p(0, "vv")
        h_groups(0, 0)
        h_groups(1, 0)
        h_copy(0, 0)
        h_copy(1, 0)
        g_w = c_unit(w_t(0))
        w_p(1, "vv")
        w_q(0, g_w)
        h_groups(0, 1)
        h_copy(0, 1)
        g_w = c_unit(w_t(1))
        h_groups(1, 1)
        h_copy(1, 1)
        w_q(1, g_w)
        sort_b(0, "vs")
        sort_b(1)
        coefficients()
        nc.vector.quantize_mx(out=hq[:].bitcast(FP8X4), scales=hs[:], in_=hg[:])
        accs = [base(0, 0), base(0, 1)]
        for lp in range(4):
            b_t(lp, "sv"[lp // 2])
        accs.append(base(0, 2))
        w_p(2, "sv")
        for lp in range(4, 8):
            b_t(lp, "sv"[lp // 2 - 2])
        accs.append(base(0, 3, cs=(0, 1)))
        w_p(3, "sv")
        b_scale(0)
        g_w = c_unit(w_t(2))
        base(0, 3, accs[3], (2, 3))
        b_quant(0)
        w_q(2, g_w)
        w_p(4, "sv")
        g_w = c_unit(w_t(3))
        lora(0, 0, accs[0])
        lora(0, 1, accs[1])
        fin(0, 0, accs[0])
        w_q(3, g_w)
        fin(0, 1, accs[1])
        w_p(5, "vv")
        g_w = g_tile()
        c_unit(w_t(4, (0, 1)), "ss", g_w, (0, 1))
        lora(0, 2, accs[2])
        lora(0, 3, accs[3])
        c_unit(w_t(4, (2, 3)), "ss", g_w, (2, 3))
        for tt in range(2, 4):
            fin(0, tt, accs[tt])
        w_q(4, g_w)
        b_scale(1)
        for m in range(2, 8):
            g = m // 2
            k = m + 3
            if k + 1 < 8:
                w_p(k + 1, "sv")
            g_w = g_tile() if k < 8 else None
            for j in range(2):
                tt = 2 * (m % 2) + j
                if (m, j) == (7, 1):
                    last_tile(g, tt)
                    continue
                acc = base(g, tt)
                lora(g, tt, acc)
                cs = (2 * j, 2 * j + 1)
                if k < 8:
                    c_unit(w_t(k, cs), "ss", g_w, cs)
                fin(g, tt, acc)
                if (m, j) == (2, 1):
                    b_quant(1)
                if k < 8:
                    w_q(k, g_w, cs)
